import numpy as np
import ml_dtypes


def mxq(x, axis, fmt="e4m3"):
    dtype, down = {"e4m3": (ml_dtypes.float8_e4m3fn, 7), "e5m2": (ml_dtypes.float8_e5m2, 14)}[fmt]
    v = np.moveaxis(np.asarray(x, np.float32).astype(ml_dtypes.bfloat16).astype(np.float64), axis, -1)
    blocks = v.reshape(v.shape[:-1] + (-1, 32))
    amax = np.abs(blocks).max(-1, keepdims=True)
    byte = np.maximum(np.where(amax > 0, np.frexp(amax)[1] - 1 + 127, 0) - down, 1)
    scale = np.exp2(byte - 127.0)
    codes = (blocks / scale).astype(np.float32).astype(dtype).astype(np.float64)
    return np.moveaxis((codes * scale).reshape(v.shape), -1, axis)


WIDE = False


def mx_kscale(k):
    if not WIDE:
        return np.ones(k)
    levels = np.array([10, -10, 5, -5, 0])
    if k % 512:
        return np.exp2(np.random.permutation(np.resize(levels, k // 32))).repeat(32)
    a = np.empty((k // 512, 16))
    for p in range(k // 512):
        a[p, :8] = np.random.permutation(np.resize(levels, 8))
        for g in range(8):
            far = levels[np.abs(levels - a[p, g]) >= 10]
            a[p, g + 8] = far[np.random.randint(len(far))]
    return np.exp2(a.ravel()).repeat(32)


BF16 = ml_dtypes.bfloat16


def bf(x):
    return np.asarray(x, np.float32).astype(BF16)


def f64(x):
    return np.asarray(x).astype(np.float64)


B, S, D, H, DH = 2, 256, 2048, 16, 128
ROPE_BASE = 10000.0


def rope_tables():
    inv_freq = 1.0 / (ROPE_BASE ** (f64(np.arange(0, DH, 2)) / DH))
    freqs = f64(np.arange(S))[:, None] * inv_freq[None, :]
    return np.cos(freqs), np.sin(freqs)


def rope_interleaved(t, cos, sin):
    x1 = t[..., 0::2]
    x2 = t[..., 1::2]
    c = cos[None, :, None, :]
    s_ = sin[None, :, None, :]
    even = x1 * c - x2 * s_
    odd = x1 * s_ + x2 * c
    return np.stack((even, odd), axis=-1).reshape(t.shape)


def setup_inputs():
    s = mx_kscale(D)
    return {"x": bf(np.random.standard_normal((B, S, D)) * s),
            "wqk_w": bf(np.random.standard_normal((2 * H * DH, D)) / np.sqrt(D) / s[None, :])}


def reference(x, wqk_w):
    xqk = (mxq(f64(x), 2, "e4m3") @ mxq(f64(wqk_w), 1, "e4m3").T).reshape(B, S, 2, H, DH)
    cos, sin = rope_tables()
    q = rope_interleaved(xqk[:, :, 0], cos, sin).transpose(0, 2, 1, 3)
    k = rope_interleaved(xqk[:, :, 1], cos, sin).transpose(0, 2, 1, 3)
    return q, k

@@ -1,0 +1,242 @@
+import math
+from contextlib import ExitStack
+
+import concourse.mybir as mybir
+from concourse.masks import make_identity
+
+F32 = mybir.dt.float32
+BF16 = mybir.dt.bfloat16
+I32 = mybir.dt.int32
+U32 = mybir.dt.uint32
+U8 = mybir.dt.uint8
+FP8X4 = mybir.dt.float8_e4m3fn_x4
+ALU = mybir.AluOpType
+ACT = mybir.ActivationFunctionType
+
+P = 128
+BATCH, SEQ, D_MODEL, HEADS, D_HEAD = 2, 256, 2048, 16, 128
+ROPE_BASE = 10000.0
+PAIRS = D_HEAD // 2
+K_PASS = 4 * P
+PASSES = D_MODEL // K_PASS
+ROW_WORDS = D_MODEL // 2
+PASS_WORDS = K_PASS // 2
+BLOCKS = 4
+CHUNK = BLOCKS * P
+W_CHUNKS = 2 * HEADS * D_HEAD // CHUNK
+CHUNKS_PER_OUTPUT = W_CHUNKS // 2
+HALF_WORDS = ROW_WORDS // 2
+W_HALVES = 2 * W_CHUNKS
+W_BUFS = 10
+AHEAD = 2
+ROUND_MAGIC = 1.5 * 2.0**23
+COS, SIN = 0, 1
+
+FLOPS = 2 * BATCH * SEQ * D_MODEL * 2 * HEADS * D_HEAD
+
+
+def build_rotation_tables(nc, consts):
+    position_int = consts.tile([P, 2], I32)
+    nc.gpsimd.iota(position_int[:], pattern=[[1, 2]], base=0, channel_multiplier=2)
+    position = consts.tile([P, 2], F32)
+    nc.vector.tensor_copy(out=position[:], in_=position_int[:])
+
+    freq = consts.tile([P, PAIRS], F32)
+    nc.vector.memset(freq[:, 0:1], 1.0)
+    width = 1
+    while width < PAIRS:
+        nc.vector.tensor_scalar_mul(
+            out=freq[:, width : 2 * width],
+            in0=freq[:, 0:width],
+            scalar1=ROPE_BASE ** (-width / PAIRS),
+        )
+        width *= 2
+
+    turns = consts.tile([P, 2, 2, PAIRS], F32)
+    for a in range(2):
+        nc.vector.tensor_scalar(
+            out=turns[:, a, SIN, :],
+            in0=freq[:],
+            scalar1=position[:, a : a + 1],
+            scalar2=1.0 / (2.0 * math.pi),
+            op0=ALU.mult,
+            op1=ALU.mult,
+        )
+    nc.vector.tensor_scalar_add(out=turns[:, :, COS, :], in0=turns[:, :, SIN, :], scalar1=0.25)
+
+    flat_turns = turns[:].rearrange("p a k i -> p (a k i)")
+    rounded = consts.tile([P, 4 * PAIRS], F32)
+    nc.vector.tensor_scalar_add(out=rounded[:], in0=flat_turns, scalar1=ROUND_MAGIC)
+    excess = consts.tile([P, 2, 2, PAIRS], F32)
+    nc.vector.scalar_tensor_tensor(
+        out=excess[:].rearrange("p a k i -> p (a k i)"),
+        in0=rounded[:],
+        scalar=ROUND_MAGIC,
+        in1=flat_turns,
+        op0=ALU.subtract,
+        op1=ALU.subtract,
+    )
+
+    factors = consts.tile([P, 2, 2, PAIRS, 2], F32)
+    nc.scalar.activation(
+        out=factors[:, :, 0, :, :],
+        in_=excess[:].rearrange("p a k i -> p a i k"),
+        func=ACT.Sin,
+        scale=-2.0 * math.pi,
+    )
+    nc.scalar.activation(
+        out=factors[:, :, 1, :, 0], in_=excess[:, :, SIN, :], func=ACT.Sin, scale=2.0 * math.pi
+    )
+    nc.scalar.activation(
+        out=factors[:, :, 1, :, 1], in_=excess[:, :, COS, :], func=ACT.Sin, scale=-2.0 * math.pi
+    )
+    return factors
+
+
+def tile_attention_pa_kernel(tc, x, wqk_w, out_0, out_1):
+    nc = tc.nc
+    with ExitStack() as stack:
+        consts = stack.enter_context(tc.tile_pool(name="consts", bufs=1))
+        w_pool = stack.enter_context(tc.tile_pool(name="w_rows", bufs=W_BUFS))
+        grouped_pool = stack.enter_context(tc.tile_pool(name="grouped", bufs=3))
+        w_mx_pool = stack.enter_context(tc.tile_pool(name="w_mx", bufs=2))
+        rope_pool = stack.enter_context(tc.tile_pool(name="rope", bufs=4))
+        transposed_pool = stack.enter_context(tc.psum_pool(name="transposed", bufs=4))
+        sums_pool = stack.enter_context(tc.psum_pool(name="sums", bufs=4))
+        stack.enter_context(tc.manual_schedule())
+
+        def load_w_half(j):
+            c, pass_pair = divmod(j, 2)
+            w_half = w_pool.tile([P, BLOCKS * 2 * K_PASS], BF16)
+            nc.sync.dma_start(
+                out=w_half[:].rearrange("p (r k) -> p r k", r=BLOCKS),
+                in_=wqk_w[
+                    c * CHUNK : (c + 1) * CHUNK, pass_pair * 2 * K_PASS : (pass_pair + 1) * 2 * K_PASS
+                ].rearrange("(r p) k -> p r k", p=P),
+            )
+            return w_half[:].bitcast(F32).rearrange("p (r w) -> p r w", r=BLOCKS)
+
+        def transpose_two_passes(half_rows, vector_helps):
+            grouped = grouped_pool.tile([P, 2 * 4 * CHUNK], BF16, align_bytes=64)
+            grouped_words = grouped[:].bitcast(F32).rearrange(
+                "p (g r c u) -> p g r c u", g=2, r=BLOCKS, u=2
+            )
+            for g in range(2):
+                for first_block in range(0, BLOCKS, 2):
+                    bank = transposed_pool.tile([P, 2, 2, P], F32)
+                    for r in range(2):
+                        for u in range(2):
+                            words = slice(g * PASS_WORDS + u, (g + 1) * PASS_WORDS, 2)
+                            nc.tensor.transpose(
+                                bank[:, r, u, :],
+                                half_rows[:, first_block + r, words],
+                                identity[:],
+                            )
+                    side_by_side = grouped_words[:, g, first_block : first_block + 2, :, :]
+                    by_column = bank[:].rearrange("p r u c -> p r c u")
+                    if vector_helps and first_block > 0:
+                        nc.vector.tensor_copy(out=side_by_side, in_=by_column)
+                    else:
+                        nc.scalar.copy(out=side_by_side, in_=by_column)
+            return grouped
+
+        def quantise_two_passes(grouped, codes, scales, pass_pair):
+            passes = slice(2 * pass_pair, 2 * pass_pair + 2)
+            nc.vector.quantize_mx(
+                out=codes[:, passes, :].rearrange("p g n -> p (g n)").bitcast(FP8X4),
+                scales=scales[:, passes, :].rearrange("p g n -> p (g n)"),
+                in_=grouped[:],
+            )
+
+        def project(token_tile, w_codes, w_scales):
+            tokens = slice(token_tile * P, (token_tile + 1) * P)
+            sums = sums_pool.tile([P, CHUNK], F32)
+            for g in range(PASSES):
+                nc.tensor.matmul_mx(
+                    out=sums[:],
+                    lhsT=x_codes[:, g, tokens].bitcast(FP8X4),
+                    lhsT_scale=x_scales[:, g, tokens],
+                    rhs=w_codes[:, g, :].bitcast(FP8X4),
+                    rhs_scale=w_scales[:, g, :],
+                    start=(g == 0),
+                    stop=(g == PASSES - 1),
+                )
+            return sums
+
+        def rotate(sums, a, rotated):
+            shape = [P, 2, BLOCKS, PAIRS, 2]
+            products = rope_pool.tile(shape, F32)
+            nc.vector.tensor_tensor(
+                out=products[:],
+                in0=sums[:]
+                .rearrange("p (h i k) -> p k h i", h=BLOCKS, k=2)
+                .unsqueeze(4)
+                .to_broadcast(shape),
+                in1=factors[:, a, :, :, :].unsqueeze(2).to_broadcast(shape),
+                op=ALU.mult,
+            )
+            nc.gpsimd.tensor_tensor(
+                out=rotated[:, :, a, :],
+                in0=products[:, 0, :, :, :].rearrange("p h i e -> p h (i e)"),
+                in1=products[:, 1, :, :, :].rearrange("p h i e -> p h (i e)"),
+                op=ALU.add,
+            )
+
+        def store(rotated, c, b):
+            output = out_0 if c < CHUNKS_PER_OUTPUT else out_1
+            first_head = (c % CHUNKS_PER_OUTPUT) * BLOCKS
+            nc.sync.dma_start(
+                out=output[b, first_head : first_head + BLOCKS, :, :].rearrange(
+                    "h (m a) j -> m h (a j)", a=2
+                ),
+                in_=rotated[:].rearrange("p h a j -> p h (a j)"),
+            )
+
+        x_rows = consts.tile([P, BLOCKS * D_MODEL], BF16)
+        for b in range(BATCH):
+            nc.sync.dma_start(
+                out=x_rows[:, 2 * b * D_MODEL : 2 * (b + 1) * D_MODEL],
+                in_=x[b, :, :].rearrange("(m a) k -> m (a k)", a=2),
+            )
+        w_half_of = {j: load_w_half(j) for j in range(W_BUFS)}
+
+        identity = consts.tile([P, P], F32)
+        make_identity(nc, identity[:])
+        factors = build_rotation_tables(nc, consts)
+
+        x_words = x_rows[:].bitcast(F32).rearrange("p (r w) -> p r w", r=BLOCKS)
+        x_codes = consts.tile([P, PASSES, CHUNK], U32, align_bytes=64)
+        x_scales = consts.tile([P, PASSES, CHUNK], U8, align_bytes=64)
+        for pass_pair in range(2):
+            half_rows = x_words[:, :, pass_pair * HALF_WORDS : (pass_pair + 1) * HALF_WORDS]
+            grouped = transpose_two_passes(half_rows, vector_helps=True)
+            quantise_two_passes(grouped, x_codes, x_scales, pass_pair)
+
+        w_mx_of = {}
+
+        def new_w_mx(c):
+            w_codes = w_mx_pool.tile([P, PASSES, CHUNK], U32, align_bytes=64)
+            w_scales = w_mx_pool.tile([P, PASSES, CHUNK], U8, align_bytes=64)
+            w_mx_of[c] = (w_codes, w_scales)
+
+        new_w_mx(0)
+        for j in range(AHEAD):
+            grouped = transpose_two_passes(w_half_of[j], vector_helps=True)
+            quantise_two_passes(grouped, w_mx_of[0][0], w_mx_of[0][1], j)
+
+        for k in range(W_HALVES):
+            c, b = divmod(k, 2)
+            if k + W_BUFS < W_HALVES:
+                w_half_of[k + W_BUFS] = load_w_half(k + W_BUFS)
+            j = k + AHEAD
+            if j < W_HALVES:
+                if j % 2 == 0:
+                    new_w_mx(j // 2)
+                grouped = transpose_two_passes(w_half_of[j], vector_helps=False)
+            sums_of = {a: project(2 * b + a, w_mx_of[c][0], w_mx_of[c][1]) for a in range(2)}
+            rotated = rope_pool.tile([P, BLOCKS, 2, D_HEAD], F32)
+            rotate(sums_of[0], 0, rotated)
+            if j < W_HALVES:
+                quantise_two_passes(grouped, w_mx_of[j // 2][0], w_mx_of[j // 2][1], j % 2)
+            rotate(sums_of[1], 1, rotated)
+            store(rotated, c, b)

@@ -21,21 +21,21 @@ K_PASS = 4 * P
 PASSES = D_MODEL // K_PASS
 ROW_WORDS = D_MODEL // 2
 PASS_WORDS = K_PASS // 2
-BLOCKS = 4
-CHUNK = BLOCKS * P
-W_CHUNKS = 2 * HEADS * D_HEAD // CHUNK
-CHUNKS_PER_OUTPUT = W_CHUNKS // 2
-HALF_WORDS = ROW_WORDS // 2
-W_HALVES = 2 * W_CHUNKS
-W_BUFS = 10
-AHEAD = 2
+SORTED_PASSES = 3
+RUN_WORDS = 8
+RUNS = PASS_WORDS // (2 * RUN_WORDS)
+UNIT = 2 * P
+UNIT_HEADS = UNIT // D_HEAD
+W_UNITS = 2 * HEADS // UNIT_HEADS
+UNITS_PER_OUTPUT = W_UNITS // 2
+UNIT_BUFS = 11
 ROUND_MAGIC = 1.5 * 2.0**23
 COS, SIN = 0, 1
 
 FLOPS = 2 * BATCH * SEQ * D_MODEL * 2 * HEADS * D_HEAD
 
 
-def build_rotation_tables(nc, consts):
+def build_angles(nc, consts):
     position_int = consts.tile([P, 2], I32)
     nc.gpsimd.iota(position_int[:], pattern=[[1, 2]], base=0, channel_multiplier=2)
     position = consts.tile([P, 2], F32)
@@ -76,19 +76,22 @@ def build_rotation_tables(nc, consts):
         op0=ALU.subtract,
         op1=ALU.subtract,
     )
+    return excess
 
+
+def build_factors(nc, consts, excess):
     factors = consts.tile([P, 2, 2, PAIRS, 2], F32)
     nc.scalar.activation(
-        out=factors[:, :, 0, :, :],
+        out=factors[:, 0, :, :, :],
         in_=excess[:].rearrange("p a k i -> p a i k"),
         func=ACT.Sin,
         scale=-2.0 * math.pi,
     )
     nc.scalar.activation(
-        out=factors[:, :, 1, :, 0], in_=excess[:, :, SIN, :], func=ACT.Sin, scale=2.0 * math.pi
+        out=factors[:, 1, :, :, 0], in_=excess[:, :, SIN, :], func=ACT.Sin, scale=2.0 * math.pi
     )
     nc.scalar.activation(
-        out=factors[:, :, 1, :, 1], in_=excess[:, :, COS, :], func=ACT.Sin, scale=-2.0 * math.pi
+        out=factors[:, 1, :, :, 1], in_=excess[:, :, COS, :], func=ACT.Sin, scale=-2.0 * math.pi
     )
     return factors
 
@@ -97,146 +100,202 @@ def tile_attention_pa_kernel(tc, x, wqk_w, out_0, out_1):
     nc = tc.nc
     with ExitStack() as stack:
         consts = stack.enter_context(tc.tile_pool(name="consts", bufs=1))
-        w_pool = stack.enter_context(tc.tile_pool(name="w_rows", bufs=W_BUFS))
+        rows_pool = stack.enter_context(tc.tile_pool(name="rows", bufs=UNIT_BUFS))
+        sorted_pool = stack.enter_context(tc.tile_pool(name="sorted", bufs=3))
         grouped_pool = stack.enter_context(tc.tile_pool(name="grouped", bufs=3))
-        w_mx_pool = stack.enter_context(tc.tile_pool(name="w_mx", bufs=2))
+        mx_pool = stack.enter_context(tc.tile_pool(name="mx", bufs=4))
         rope_pool = stack.enter_context(tc.tile_pool(name="rope", bufs=4))
+        rotated_pool = stack.enter_context(tc.tile_pool(name="rotated", bufs=8))
         transposed_pool = stack.enter_context(tc.psum_pool(name="transposed", bufs=4))
         sums_pool = stack.enter_context(tc.psum_pool(name="sums", bufs=4))
         stack.enter_context(tc.manual_schedule())
 
-        def load_w_half(j):
-            c, pass_pair = divmod(j, 2)
-            w_half = w_pool.tile([P, BLOCKS * 2 * K_PASS], BF16)
-            nc.sync.dma_start(
-                out=w_half[:].rearrange("p (r k) -> p r k", r=BLOCKS),
-                in_=wqk_w[
-                    c * CHUNK : (c + 1) * CHUNK, pass_pair * 2 * K_PASS : (pass_pair + 1) * 2 * K_PASS
-                ].rearrange("(r p) k -> p r k", p=P),
-            )
-            return w_half[:].bitcast(F32).rearrange("p (r w) -> p r w", r=BLOCKS)
+        def load(source, dmas):
+            rows = rows_pool.tile([P, 2, D_MODEL], BF16)
+            if dmas == 1:
+                nc.sync.dma_start(out=rows[:], in_=source.rearrange("r p k -> p r k"))
+            else:
+                for r in range(2):
+                    nc.sync.dma_start(out=rows[:, r, :], in_=source[r, :, :])
+            return rows
 
-        def transpose_two_passes(half_rows, vector_helps):
-            grouped = grouped_pool.tile([P, 2 * 4 * CHUNK], BF16, align_bytes=64)
-            grouped_words = grouped[:].bitcast(F32).rearrange(
-                "p (g r c u) -> p g r c u", g=2, r=BLOCKS, u=2
+        def load_x(b, dmas):
+            return load(x[b, :, :].rearrange("(m a) k -> a m k", a=2), dmas)
+
+        def load_w(j, dmas):
+            return load(
+                wqk_w[j * UNIT : (j + 1) * UNIT, :].rearrange("(r p) k -> r p k", p=P), dmas
             )
-            for g in range(2):
-                for first_block in range(0, BLOCKS, 2):
+
+        def sort(rows, engines):
+            sorted_words = []
+            for r in range(2):
+                part = sorted_pool.tile([P, 2, SORTED_PASSES * RUNS, RUN_WORDS], F32, name=f"sorted_{r}")
+                words = rows[:, r, :].bitcast(F32)[:, 0 : SORTED_PASSES * PASS_WORDS]
+                words = words.rearrange("p (w u i) -> p u w i", u=2, i=RUN_WORDS)
+                if engines[r] == "vector":
+                    nc.vector.tensor_copy(out=part[:], in_=words)
+                else:
+                    nc.scalar.copy(out=part[:], in_=words)
+                sorted_words.append(part)
+            return sorted_words
+
+        def transpose(rows, sorted_words, vector_banks=()):
+            grouped = grouped_pool.tile([P, PASSES * UNIT * 4], BF16, align_bytes=64)
+            grouped_words = grouped[:].bitcast(F32).rearrange(
+                "p (g r c u) -> p g r c u", g=PASSES, r=2, u=2
+            )
+            for r in range(2):
+                words = rows[:, r, :].bitcast(F32)
+                for first in range(0, PASSES, 2):
                     bank = transposed_pool.tile([P, 2, 2, P], F32)
-                    for r in range(2):
+                    for g in range(first, first + 2):
                         for u in range(2):
-                            words = slice(g * PASS_WORDS + u, (g + 1) * PASS_WORDS, 2)
-                            nc.tensor.transpose(
-                                bank[:, r, u, :],
-                                half_rows[:, first_block + r, words],
-                                identity[:],
-                            )
-                    side_by_side = grouped_words[:, g, first_block : first_block + 2, :, :]
-                    by_column = bank[:].rearrange("p r u c -> p r c u")
-                    if vector_helps and first_block > 0:
+                            if g < SORTED_PASSES:
+                                operand = sorted_words[r][:, u, RUNS * g : RUNS * (g + 1), :].rearrange(
+                                    "p w i -> p (w i)"
+                                )
+                            else:
+                                operand = words[:, PASS_WORDS * g + u : PASS_WORDS * (g + 1) : 2]
+                            nc.tensor.transpose(bank[:, g - first, u, :], operand, identity[:])
+                    side_by_side = grouped_words[:, first : first + 2, r, :, :]
+                    by_column = bank[:].rearrange("p g u c -> p g c u")
+                    if 2 * r + first // 2 in vector_banks:
                         nc.vector.tensor_copy(out=side_by_side, in_=by_column)
                     else:
                         nc.scalar.copy(out=side_by_side, in_=by_column)
             return grouped
 
-        def quantise_two_passes(grouped, codes, scales, pass_pair):
-            passes = slice(2 * pass_pair, 2 * pass_pair + 2)
+        def quantise(grouped, pool, name):
+            codes = pool.tile([P, PASSES, UNIT], U32, align_bytes=64, name=f"codes_{name}")
+            scales = pool.tile([P, PASSES, UNIT], U8, align_bytes=64, name=f"scales_{name}")
             nc.vector.quantize_mx(
-                out=codes[:, passes, :].rearrange("p g n -> p (g n)").bitcast(FP8X4),
-                scales=scales[:, passes, :].rearrange("p g n -> p (g n)"),
+                out=codes[:].rearrange("p g n -> p (g n)").bitcast(FP8X4),
+                scales=scales[:].rearrange("p g n -> p (g n)"),
                 in_=grouped[:],
             )
+            return codes, scales
 
-        def project(token_tile, w_codes, w_scales):
-            tokens = slice(token_tile * P, (token_tile + 1) * P)
-            sums = sums_pool.tile([P, CHUNK], F32)
-            for g in range(PASSES):
-                nc.tensor.matmul_mx(
-                    out=sums[:],
-                    lhsT=x_codes[:, g, tokens].bitcast(FP8X4),
-                    lhsT_scale=x_scales[:, g, tokens],
-                    rhs=w_codes[:, g, :].bitcast(FP8X4),
-                    rhs_scale=w_scales[:, g, :],
-                    start=(g == 0),
-                    stop=(g == PASSES - 1),
-                )
+        def project(b, w_mx):
+            sums = sums_pool.tile([P, 2, UNIT], F32)
+            x_codes, x_scales = x_mx_of[b]
+            w_codes, w_scales = w_mx
+            for a in range(2):
+                tokens = slice(a * P, (a + 1) * P)
+                for g in range(PASSES):
+                    nc.tensor.matmul_mx(
+                        out=sums[:, a, :],
+                        lhsT=x_codes[:, g, tokens].bitcast(FP8X4),
+                        lhsT_scale=x_scales[:, g, tokens],
+                        rhs=w_codes[:, g, :].bitcast(FP8X4),
+                        rhs_scale=w_scales[:, g, :],
+                        start=(g == 0),
+                        stop=(g == PASSES - 1),
+                    )
             return sums
 
-        def rotate(sums, a, rotated):
-            shape = [P, 2, BLOCKS, PAIRS, 2]
+        def multiply(sums):
+            shape = [P, 2, 2, UNIT_HEADS, PAIRS, 2]
             products = rope_pool.tile(shape, F32)
             nc.vector.tensor_tensor(
                 out=products[:],
                 in0=sums[:]
-                .rearrange("p (h i k) -> p k h i", h=BLOCKS, k=2)
-                .unsqueeze(4)
+                .rearrange("p a (h i k) -> p k a h i", h=UNIT_HEADS, k=2)
+                .unsqueeze(5)
                 .to_broadcast(shape),
-                in1=factors[:, a, :, :, :].unsqueeze(2).to_broadcast(shape),
+                in1=factors[:].unsqueeze(3).to_broadcast(shape),
                 op=ALU.mult,
             )
-            nc.gpsimd.tensor_tensor(
-                out=rotated[:, :, a, :],
-                in0=products[:, 0, :, :, :].rearrange("p h i e -> p h (i e)"),
-                in1=products[:, 1, :, :, :].rearrange("p h i e -> p h (i e)"),
+            return products
+
+        def add(engine, products, rotated, heads):
+            terms = products[:, :, :, heads.start : heads.stop, :, :]
+            engine.tensor_tensor(
+                out=rotated[:, heads.start : heads.stop, :, :].rearrange("p h a j -> p a h j"),
+                in0=terms[:, 0, :, :, :, :].rearrange("p a h i e -> p a h (i e)"),
+                in1=terms[:, 1, :, :, :, :].rearrange("p a h i e -> p a h (i e)"),
                 op=ALU.add,
             )
 
-        def store(rotated, c, b):
-            output = out_0 if c < CHUNKS_PER_OUTPUT else out_1
-            first_head = (c % CHUNKS_PER_OUTPUT) * BLOCKS
+        def store(rotated, j, b, heads):
+            output = out_0 if j < UNITS_PER_OUTPUT else out_1
+            first_head = (j % UNITS_PER_OUTPUT) * UNIT_HEADS
             nc.sync.dma_start(
-                out=output[b, first_head : first_head + BLOCKS, :, :].rearrange(
+                out=output[b, first_head + heads.start : first_head + heads.stop, :, :].rearrange(
                     "h (m a) j -> m h (a j)", a=2
                 ),
-                in_=rotated[:].rearrange("p h a j -> p h (a j)"),
+                in_=rotated[:, heads.start : heads.stop, :, :].rearrange("p h a j -> p h (a j)"),
             )
 
-        x_rows = consts.tile([P, BLOCKS * D_MODEL], BF16)
-        for b in range(BATCH):
-            nc.sync.dma_start(
-                out=x_rows[:, 2 * b * D_MODEL : 2 * (b + 1) * D_MODEL],
-                in_=x[b, :, :].rearrange("(m a) k -> m (a k)", a=2),
-            )
-        w_half_of = {j: load_w_half(j) for j in range(W_BUFS)}
+        x_rows_of = {0: load_x(0, dmas=2)}
+        w_rows_of = {0: load_w(0, dmas=2)}
+        x_rows_of[1] = load_x(1, dmas=2)
+        for j in range(1, UNIT_BUFS - 2):
+            w_rows_of[j] = load_w(j, dmas=1)
+
+        warm = consts.tile([P, 1], F32)
+        nc.vector.memset(warm[:], 0.0)
+        nc.scalar.activation(out=warm[:], in_=warm[:], func=ACT.Sin)
 
         identity = consts.tile([P, P], F32)
         make_identity(nc, identity[:])
-        factors = build_rotation_tables(nc, consts)
+        excess = build_angles(nc, consts)
 
-        x_words = x_rows[:].bitcast(F32).rearrange("p (r w) -> p r w", r=BLOCKS)
-        x_codes = consts.tile([P, PASSES, CHUNK], U32, align_bytes=64)
-        x_scales = consts.tile([P, PASSES, CHUNK], U8, align_bytes=64)
-        for pass_pair in range(2):
-            half_rows = x_words[:, :, pass_pair * HALF_WORDS : (pass_pair + 1) * HALF_WORDS]
-            grouped = transpose_two_passes(half_rows, vector_helps=True)
-            quantise_two_passes(grouped, x_codes, x_scales, pass_pair)
-
+        both_heads = range(UNIT_HEADS)
+        x_mx_of = {}
         w_mx_of = {}
+        w_sorted_of = {}
 
-        def new_w_mx(c):
-            w_codes = w_mx_pool.tile([P, PASSES, CHUNK], U32, align_bytes=64)
-            w_scales = w_mx_pool.tile([P, PASSES, CHUNK], U8, align_bytes=64)
-            w_mx_of[c] = (w_codes, w_scales)
+        def sort_and_transpose(rows, engines=("vector", "vector")):
+            return transpose(rows, sort(rows, engines))
 
-        new_w_mx(0)
-        for j in range(AHEAD):
-            grouped = transpose_two_passes(w_half_of[j], vector_helps=True)
-            quantise_two_passes(grouped, w_mx_of[0][0], w_mx_of[0][1], j)
+        def rotate(sums, j, b):
+            rotated = rotated_pool.tile([P, UNIT_HEADS, 2, D_HEAD], F32)
+            add(nc.gpsimd, multiply(sums), rotated, both_heads)
+            store(rotated, j, b, both_heads)
 
-        for k in range(W_HALVES):
-            c, b = divmod(k, 2)
-            if k + W_BUFS < W_HALVES:
-                w_half_of[k + W_BUFS] = load_w_half(k + W_BUFS)
-            j = k + AHEAD
-            if j < W_HALVES:
-                if j % 2 == 0:
-                    new_w_mx(j // 2)
-                grouped = transpose_two_passes(w_half_of[j], vector_helps=False)
-            sums_of = {a: project(2 * b + a, w_mx_of[c][0], w_mx_of[c][1]) for a in range(2)}
-            rotated = rope_pool.tile([P, BLOCKS, 2, D_HEAD], F32)
-            rotate(sums_of[0], 0, rotated)
-            if j < W_HALVES:
-                quantise_two_passes(grouped, w_mx_of[j // 2][0], w_mx_of[j // 2][1], j % 2)
-            rotate(sums_of[1], 1, rotated)
-            store(rotated, c, b)
+        grouped_x = sort_and_transpose(x_rows_of[0], ("scalar", "vector"))
+        grouped = sort_and_transpose(w_rows_of[0])
+        x_mx_of[0] = quantise(grouped_x, consts, "x_0")
+        grouped_x = sort_and_transpose(x_rows_of[1])
+        w_mx_of[0] = quantise(grouped, mx_pool, "w")
+        factors = build_factors(nc, consts, excess)
+        sums = project(0, w_mx_of[0])
+        w_sorted_of[1] = sort(w_rows_of[1], ("vector", "vector"))
+        x_mx_of[1] = quantise(grouped_x, consts, "x_1")
+        grouped = transpose(w_rows_of[1], w_sorted_of[1])
+        rotate(sums, 0, 0)
+        sums = project(1, w_mx_of[0])
+        w_sorted_of[2] = sort(w_rows_of[2], ("vector", "scalar"))
+        w_mx_of[1] = quantise(grouped, mx_pool, "w")
+        rotate(sums, 0, 1)
+        grouped = transpose(w_rows_of[2], w_sorted_of[2])
+        w_sorted_of[3] = sort(w_rows_of[3], ("vector", "scalar"))
+
+        for k in range(1, W_UNITS):
+            if k + UNIT_BUFS - 3 < W_UNITS:
+                w_rows_of[k + UNIT_BUFS - 3] = load_w(k + UNIT_BUFS - 3, dmas=1)
+            ahead = k + 2
+            if k == 2:
+                grouped = transpose(w_rows_of[3], w_sorted_of[3])
+                w_mx_of[3] = quantise(grouped, mx_pool, "w")
+            if k > 1 and ahead < W_UNITS:
+                grouped = transpose(w_rows_of[ahead], w_sorted_of[ahead])
+                if ahead + 1 < W_UNITS:
+                    w_sorted_of[ahead + 1] = sort(w_rows_of[ahead + 1], ("scalar", "scalar"))
+            sums_of = [project(b, w_mx_of[k]) for b in range(BATCH)]
+            rotate(sums_of[0], k, 0)
+            if k == 1:
+                w_mx_of[2] = quantise(grouped, mx_pool, "w")
+                w_sorted_of[4] = sort(w_rows_of[4], ("vector", "vector"))
+            elif ahead < W_UNITS:
+                w_mx_of[ahead] = quantise(grouped, mx_pool, "w")
+            if k < W_UNITS - 1:
+                rotate(sums_of[1], k, 1)
+            else:
+                rotated = rotated_pool.tile([P, UNIT_HEADS, 2, D_HEAD], F32)
+                products = multiply(sums_of[1])
+                for h in range(UNIT_HEADS):
+                    head = range(h, h + 1)
+                    add(nc.vector, products, rotated, head)
+                    store(rotated, k, 1, head)

import math
from contextlib import ExitStack

import concourse.mybir as mybir
from concourse.masks import make_identity

F32 = mybir.dt.float32
BF16 = mybir.dt.bfloat16
I32 = mybir.dt.int32
U32 = mybir.dt.uint32
U8 = mybir.dt.uint8
FP8X4 = mybir.dt.float8_e4m3fn_x4
ALU = mybir.AluOpType
ACT = mybir.ActivationFunctionType

P = 128
BATCH, SEQ, D_MODEL, HEADS, D_HEAD = 2, 256, 2048, 16, 128
ROPE_BASE = 10000.0
PAIRS = D_HEAD // 2
K_PASS = 4 * P
PASSES = D_MODEL // K_PASS
ROW_WORDS = D_MODEL // 2
PASS_WORDS = K_PASS // 2
SORTED_PASSES = 3
RUN_WORDS = 8
RUNS = PASS_WORDS // (2 * RUN_WORDS)
UNIT = 2 * P
UNIT_HEADS = UNIT // D_HEAD
W_UNITS = 2 * HEADS // UNIT_HEADS
UNITS_PER_OUTPUT = W_UNITS // 2
UNIT_BUFS = 11
ROUND_MAGIC = 1.5 * 2.0**23
COS, SIN = 0, 1

FLOPS = 2 * BATCH * SEQ * D_MODEL * 2 * HEADS * D_HEAD


def build_angles(nc, consts):
    position_int = consts.tile([P, 2], I32)
    nc.gpsimd.iota(position_int[:], pattern=[[1, 2]], base=0, channel_multiplier=2)
    position = consts.tile([P, 2], F32)
    nc.vector.tensor_copy(out=position[:], in_=position_int[:])

    freq = consts.tile([P, PAIRS], F32)
    nc.vector.memset(freq[:, 0:1], 1.0)
    width = 1
    while width < PAIRS:
        nc.vector.tensor_scalar_mul(
            out=freq[:, width : 2 * width],
            in0=freq[:, 0:width],
            scalar1=ROPE_BASE ** (-width / PAIRS),
        )
        width *= 2

    turns = consts.tile([P, 2, 2, PAIRS], F32)
    for a in range(2):
        nc.vector.tensor_scalar(
            out=turns[:, a, SIN, :],
            in0=freq[:],
            scalar1=position[:, a : a + 1],
            scalar2=1.0 / (2.0 * math.pi),
            op0=ALU.mult,
            op1=ALU.mult,
        )
    nc.vector.tensor_scalar_add(out=turns[:, :, COS, :], in0=turns[:, :, SIN, :], scalar1=0.25)

    flat_turns = turns[:].rearrange("p a k i -> p (a k i)")
    rounded = consts.tile([P, 4 * PAIRS], F32)
    nc.vector.tensor_scalar_add(out=rounded[:], in0=flat_turns, scalar1=ROUND_MAGIC)
    excess = consts.tile([P, 2, 2, PAIRS], F32)
    nc.vector.scalar_tensor_tensor(
        out=excess[:].rearrange("p a k i -> p (a k i)"),
        in0=rounded[:],
        scalar=ROUND_MAGIC,
        in1=flat_turns,
        op0=ALU.subtract,
        op1=ALU.subtract,
    )
    return excess


def build_factors(nc, consts, excess):
    factors = consts.tile([P, 2, 2, PAIRS, 2], F32)
    nc.scalar.activation(
        out=factors[:, 0, :, :, :],
        in_=excess[:].rearrange("p a k i -> p a i k"),
        func=ACT.Sin,
        scale=-2.0 * math.pi,
    )
    nc.scalar.activation(
        out=factors[:, 1, :, :, 0], in_=excess[:, :, SIN, :], func=ACT.Sin, scale=2.0 * math.pi
    )
    nc.scalar.activation(
        out=factors[:, 1, :, :, 1], in_=excess[:, :, COS, :], func=ACT.Sin, scale=-2.0 * math.pi
    )
    return factors


def tile_attention_pa_kernel(tc, x, wqk_w, out_0, out_1):
    nc = tc.nc
    with ExitStack() as stack:
        consts = stack.enter_context(tc.tile_pool(name="consts", bufs=1))
        rows_pool = stack.enter_context(tc.tile_pool(name="rows", bufs=UNIT_BUFS))
        sorted_pool = stack.enter_context(tc.tile_pool(name="sorted", bufs=3))
        grouped_pool = stack.enter_context(tc.tile_pool(name="grouped", bufs=3))
        mx_pool = stack.enter_context(tc.tile_pool(name="mx", bufs=4))
        rope_pool = stack.enter_context(tc.tile_pool(name="rope", bufs=4))
        rotated_pool = stack.enter_context(tc.tile_pool(name="rotated", bufs=8))
        transposed_pool = stack.enter_context(tc.psum_pool(name="transposed", bufs=4))
        sums_pool = stack.enter_context(tc.psum_pool(name="sums", bufs=4))
        stack.enter_context(tc.manual_schedule())

        def load(source, dmas):
            rows = rows_pool.tile([P, 2, D_MODEL], BF16)
            if dmas == 1:
                nc.sync.dma_start(out=rows[:], in_=source.rearrange("r p k -> p r k"))
            else:
                for r in range(2):
                    nc.sync.dma_start(out=rows[:, r, :], in_=source[r, :, :])
            return rows

        def load_x(b, dmas):
            return load(x[b, :, :].rearrange("(m a) k -> a m k", a=2), dmas)

        def load_w(j, dmas):
            return load(
                wqk_w[j * UNIT : (j + 1) * UNIT, :].rearrange("(r p) k -> r p k", p=P), dmas
            )

        def sort(rows, engines):
            sorted_words = []
            for r in range(2):
                part = sorted_pool.tile([P, 2, SORTED_PASSES * RUNS, RUN_WORDS], F32, name=f"sorted_{r}")
                words = rows[:, r, :].bitcast(F32)[:, 0 : SORTED_PASSES * PASS_WORDS]
                words = words.rearrange("p (w u i) -> p u w i", u=2, i=RUN_WORDS)
                if engines[r] == "vector":
                    nc.vector.tensor_copy(out=part[:], in_=words)
                else:
                    nc.scalar.copy(out=part[:], in_=words)
                sorted_words.append(part)
            return sorted_words

        def transpose(rows, sorted_words, vector_banks=()):
            grouped = grouped_pool.tile([P, PASSES * UNIT * 4], BF16, align_bytes=64)
            grouped_words = grouped[:].bitcast(F32).rearrange(
                "p (g r c u) -> p g r c u", g=PASSES, r=2, u=2
            )
            for r in range(2):
                words = rows[:, r, :].bitcast(F32)
                for first in range(0, PASSES, 2):
                    bank = transposed_pool.tile([P, 2, 2, P], F32)
                    for g in range(first, first + 2):
                        for u in range(2):
                            if g < SORTED_PASSES:
                                operand = sorted_words[r][:, u, RUNS * g : RUNS * (g + 1), :].rearrange(
                                    "p w i -> p (w i)"
                                )
                            else:
                                operand = words[:, PASS_WORDS * g + u : PASS_WORDS * (g + 1) : 2]
                            nc.tensor.transpose(bank[:, g - first, u, :], operand, identity[:])
                    side_by_side = grouped_words[:, first : first + 2, r, :, :]
                    by_column = bank[:].rearrange("p g u c -> p g c u")
                    if 2 * r + first // 2 in vector_banks:
                        nc.vector.tensor_copy(out=side_by_side, in_=by_column)
                    else:
                        nc.scalar.copy(out=side_by_side, in_=by_column)
            return grouped

        def quantise(grouped, pool, name):
            codes = pool.tile([P, PASSES, UNIT], U32, align_bytes=64, name=f"codes_{name}")
            scales = pool.tile([P, PASSES, UNIT], U8, align_bytes=64, name=f"scales_{name}")
            nc.vector.quantize_mx(
                out=codes[:].rearrange("p g n -> p (g n)").bitcast(FP8X4),
                scales=scales[:].rearrange("p g n -> p (g n)"),
                in_=grouped[:],
            )
            return codes, scales

        def project(b, w_mx):
            sums = sums_pool.tile([P, 2, UNIT], F32)
            x_codes, x_scales = x_mx_of[b]
            w_codes, w_scales = w_mx
            for a in range(2):
                tokens = slice(a * P, (a + 1) * P)
                for g in range(PASSES):
                    nc.tensor.matmul_mx(
                        out=sums[:, a, :],
                        lhsT=x_codes[:, g, tokens].bitcast(FP8X4),
                        lhsT_scale=x_scales[:, g, tokens],
                        rhs=w_codes[:, g, :].bitcast(FP8X4),
                        rhs_scale=w_scales[:, g, :],
                        start=(g == 0),
                        stop=(g == PASSES - 1),
                    )
            return sums

        def multiply(sums):
            shape = [P, 2, 2, UNIT_HEADS, PAIRS, 2]
            products = rope_pool.tile(shape, F32)
            nc.vector.tensor_tensor(
                out=products[:],
                in0=sums[:]
                .rearrange("p a (h i k) -> p k a h i", h=UNIT_HEADS, k=2)
                .unsqueeze(5)
                .to_broadcast(shape),
                in1=factors[:].unsqueeze(3).to_broadcast(shape),
                op=ALU.mult,
            )
            return products

        def add(engine, products, rotated, heads):
            terms = products[:, :, :, heads.start : heads.stop, :, :]
            engine.tensor_tensor(
                out=rotated[:, heads.start : heads.stop, :, :].rearrange("p h a j -> p a h j"),
                in0=terms[:, 0, :, :, :, :].rearrange("p a h i e -> p a h (i e)"),
                in1=terms[:, 1, :, :, :, :].rearrange("p a h i e -> p a h (i e)"),
                op=ALU.add,
            )

        def store(rotated, j, b, heads):
            output = out_0 if j < UNITS_PER_OUTPUT else out_1
            first_head = (j % UNITS_PER_OUTPUT) * UNIT_HEADS
            nc.sync.dma_start(
                out=output[b, first_head + heads.start : first_head + heads.stop, :, :].rearrange(
                    "h (m a) j -> m h (a j)", a=2
                ),
                in_=rotated[:, heads.start : heads.stop, :, :].rearrange("p h a j -> p h (a j)"),
            )

        x_rows_of = {0: load_x(0, dmas=2)}
        w_rows_of = {0: load_w(0, dmas=2)}
        x_rows_of[1] = load_x(1, dmas=2)
        for j in range(1, UNIT_BUFS - 2):
            w_rows_of[j] = load_w(j, dmas=1)

        warm = consts.tile([P, 1], F32)
        nc.vector.memset(warm[:], 0.0)
        nc.scalar.activation(out=warm[:], in_=warm[:], func=ACT.Sin)

        identity = consts.tile([P, P], F32)
        make_identity(nc, identity[:])
        excess = build_angles(nc, consts)

        both_heads = range(UNIT_HEADS)
        x_mx_of = {}
        w_mx_of = {}
        w_sorted_of = {}

        def sort_and_transpose(rows, engines=("vector", "vector")):
            return transpose(rows, sort(rows, engines))

        def rotate(sums, j, b):
            rotated = rotated_pool.tile([P, UNIT_HEADS, 2, D_HEAD], F32)
            add(nc.gpsimd, multiply(sums), rotated, both_heads)
            store(rotated, j, b, both_heads)

        grouped_x = sort_and_transpose(x_rows_of[0], ("scalar", "vector"))
        grouped = sort_and_transpose(w_rows_of[0])
        x_mx_of[0] = quantise(grouped_x, consts, "x_0")
        grouped_x = sort_and_transpose(x_rows_of[1])
        w_mx_of[0] = quantise(grouped, mx_pool, "w")
        factors = build_factors(nc, consts, excess)
        sums = project(0, w_mx_of[0])
        w_sorted_of[1] = sort(w_rows_of[1], ("vector", "vector"))
        x_mx_of[1] = quantise(grouped_x, consts, "x_1")
        grouped = transpose(w_rows_of[1], w_sorted_of[1])
        rotate(sums, 0, 0)
        sums = project(1, w_mx_of[0])
        w_sorted_of[2] = sort(w_rows_of[2], ("vector", "scalar"))
        w_mx_of[1] = quantise(grouped, mx_pool, "w")
        rotate(sums, 0, 1)
        grouped = transpose(w_rows_of[2], w_sorted_of[2])
        w_sorted_of[3] = sort(w_rows_of[3], ("vector", "scalar"))

        for k in range(1, W_UNITS):
            if k + UNIT_BUFS - 3 < W_UNITS:
                w_rows_of[k + UNIT_BUFS - 3] = load_w(k + UNIT_BUFS - 3, dmas=1)
            ahead = k + 2
            if k == 2:
                grouped = transpose(w_rows_of[3], w_sorted_of[3])
                w_mx_of[3] = quantise(grouped, mx_pool, "w")
            if k > 1 and ahead < W_UNITS:
                grouped = transpose(w_rows_of[ahead], w_sorted_of[ahead])
                if ahead + 1 < W_UNITS:
                    w_sorted_of[ahead + 1] = sort(w_rows_of[ahead + 1], ("scalar", "scalar"))
            sums_of = [project(b, w_mx_of[k]) for b in range(BATCH)]
            rotate(sums_of[0], k, 0)
            if k == 1:
                w_mx_of[2] = quantise(grouped, mx_pool, "w")
                w_sorted_of[4] = sort(w_rows_of[4], ("vector", "vector"))
            elif ahead < W_UNITS:
                w_mx_of[ahead] = quantise(grouped, mx_pool, "w")
            if k < W_UNITS - 1:
                rotate(sums_of[1], k, 1)
            else:
                rotated = rotated_pool.tile([P, UNIT_HEADS, 2, D_HEAD], F32)
                products = multiply(sums_of[1])
                for h in range(UNIT_HEADS):
                    head = range(h, h + 1)
                    add(nc.vector, products, rotated, head)
                    store(rotated, k, 1, head)
